import numpy as np
import ml_dtypes

BF16 = ml_dtypes.bfloat16


def bf(x):
    return np.asarray(x, np.float32).astype(BF16)


def f32(x):
    return np.asarray(x, np.float32)


def f64(x):
    return np.asarray(x).astype(np.float64)


def striped(idx):
    return np.tile(idx.reshape(-1, 16).T, (8, 1))


D, V, N, T = 128, 2048, 1024, 2
BETA_OUT = 0.001953125
SCALE = np.sqrt(V) * ((V + T) / V) ** 1.5 * BETA_OUT


def setup_inputs():
    return {"table": bf(np.random.standard_normal((D, V))), "w": bf(np.random.standard_normal((D, D)) / np.sqrt(D)), "offs": striped(np.random.permutation(np.tile(np.arange(V), 2))[:N])}


def reference(table, w, offs):
    idx = offs[:16].T.reshape(-1)
    h = f64(w).T @ f64(table)[:, idx]
    return SCALE * (f64(table).T @ h)

@@ -1,0 +1,57 @@
+import math
+
+import concourse.mybir as mybir
+
+BF16, F32, U16 = mybir.dt.bfloat16, mybir.dt.float32, mybir.dt.uint16
+COPY = mybir.ActivationFunctionType.Copy
+
+P = 128
+V = 2048
+N = 1024
+PIECE = 512
+PIECES = N // PIECE
+BLOCKS = V // P
+SCALE = math.sqrt(V) * ((V + 2) / V) ** 1.5 / 512
+
+FLOPS = 2 * P * P * N + 2 * P * V * N
+
+
+def tile_inductionheadattentionsmaller_kernel(tc, table, w, offs, out):
+    nc = tc.nc
+    with (
+        tc.tile_pool(name="held", bufs=1) as held,
+        tc.tile_pool(name="staging", bufs=BLOCKS) as staging,
+        tc.psum_pool(name="h_banks", bufs=1) as h_banks,
+        tc.psum_pool(name="score_banks", bufs=3) as score_banks,
+    ):
+        table_sb = held.tile([P, V], BF16, name="table_sb")
+        w_sb = held.tile([P, P], BF16, name="w_sb")
+        offsets = held.tile([P, N // 16], U16, name="offsets")
+        nc.sync.dma_start(table_sb[:], table)
+        nc.sync.dma_start(offsets[:], offs)
+        nc.gpsimd.dma_start(w_sb[:], w)
+
+        def leave_psum(piece, dst, src, factor):
+            if piece % 2 == 0:
+                nc.vector.tensor_scalar_mul(dst, src, factor)
+            else:
+                nc.scalar.activation(dst, src, COPY, scale=factor)
+
+        h_bf = []
+        for piece in range(PIECES):
+            h_ps = h_banks.tile([P, PIECE], F32, name=f"h_ps{piece}")
+            piece_offsets = offsets[:, piece * (PIECE // 16) : (piece + 1) * (PIECE // 16)]
+            nc.tensor.matmul(h_ps[:], w_sb[:], table_sb[:].indirect(piece_offsets), start=True, stop=True)
+            h_piece = held.tile([P, PIECE], BF16, name=f"h_bf{piece}")
+            leave_psum(piece, h_piece[:], h_ps[:], 1.0)
+            h_bf.append(h_piece)
+
+        for block in range(BLOCKS):
+            staged = staging.tile([P, N], F32, name="staged")
+            for piece in range(PIECES):
+                scores = score_banks.tile([P, PIECE], F32, name=f"scores{piece}")
+                nc.tensor.matmul(
+                    scores[:], table_sb[:, block * P : (block + 1) * P], h_bf[piece][:], start=True, stop=True
+                )
+                leave_psum(piece, staged[:, piece * PIECE : (piece + 1) * PIECE], scores[:], SCALE)
+            nc.sync.dma_start(out[block * P : (block + 1) * P, :], staged[:])

@@ -11,6 +11,7 @@ N = 1024
 PIECE = 512
 PIECES = N // PIECE
 BLOCKS = V // P
+MAX_STORE = 4
 SCALE = math.sqrt(V) * ((V + 2) / V) ** 1.5 / 512
 
 FLOPS = 2 * P * P * N + 2 * P * V * N
@@ -20,7 +21,6 @@ def tile_inductionheadattentionsmaller_kernel(tc, table, w, offs, out):
     nc = tc.nc
     with (
         tc.tile_pool(name="held", bufs=1) as held,
-        tc.tile_pool(name="staging", bufs=BLOCKS) as staging,
         tc.psum_pool(name="h_banks", bufs=1) as h_banks,
         tc.psum_pool(name="score_banks", bufs=3) as score_banks,
     ):
@@ -28,8 +28,8 @@ def tile_inductionheadattentionsmaller_kernel(tc, table, w, offs, out):
         w_sb = held.tile([P, P], BF16, name="w_sb")
         offsets = held.tile([P, N // 16], U16, name="offsets")
         nc.sync.dma_start(table_sb[:], table)
+        nc.sync.dma_start(w_sb[:], w)
         nc.sync.dma_start(offsets[:], offs)
-        nc.gpsimd.dma_start(w_sb[:], w)
 
         def leave_psum(piece, dst, src, factor):
             if piece % 2 == 0:
@@ -46,12 +46,15 @@ def tile_inductionheadattentionsmaller_kernel(tc, table, w, offs, out):
             leave_psum(piece, h_piece[:], h_ps[:], 1.0)
             h_bf.append(h_piece)
 
+        table_blocks = table_sb[:].rearrange("k (p b) -> k b p", b=BLOCKS)
+        out_blocks = out.rearrange("(p b) n -> p b n", b=BLOCKS)
+        staged = held.tile([P, BLOCKS, N], F32, name="staged")
+        stored = 0
         for block in range(BLOCKS):
-            staged = staging.tile([P, N], F32, name="staged")
             for piece in range(PIECES):
                 scores = score_banks.tile([P, PIECE], F32, name=f"scores{piece}")
-                nc.tensor.matmul(
-                    scores[:], table_sb[:, block * P : (block + 1) * P], h_bf[piece][:], start=True, stop=True
-                )
-                leave_psum(piece, staged[:, piece * PIECE : (piece + 1) * PIECE], scores[:], SCALE)
-            nc.sync.dma_start(out[block * P : (block + 1) * P, :], staged[:])
+                nc.tensor.matmul(scores[:], table_blocks[:, block, :], h_bf[piece][:], start=True, stop=True)
+                leave_psum(piece, staged[:, block, piece * PIECE : (piece + 1) * PIECE], scores[:], SCALE)
+            if block + 1 - stored == min(max(stored, 1), MAX_STORE):
+                nc.sync.dma_start(out_blocks[:, stored : block + 1, :], staged[:, stored : block + 1, :])
+                stored = block + 1

@@ -8,10 +8,11 @@ COPY = mybir.ActivationFunctionType.Copy
 P = 128
 V = 2048
 N = 1024
-PIECE = 512
+PIECE = 256
 PIECES = N // PIECE
 BLOCKS = V // P
 MAX_STORE = 4
+PSUM_BANKS = 8
 SCALE = math.sqrt(V) * ((V + 2) / V) ** 1.5 / 512
 
 FLOPS = 2 * P * P * N + 2 * P * V * N
@@ -21,8 +22,7 @@ def tile_inductionheadattentionsmaller_kernel(tc, table, w, offs, out):
     nc = tc.nc
     with (
         tc.tile_pool(name="held", bufs=1) as held,
-        tc.psum_pool(name="h_banks", bufs=1) as h_banks,
-        tc.psum_pool(name="score_banks", bufs=3) as score_banks,
+        tc.psum_pool(name="banks", bufs=PSUM_BANKS) as banks,
     ):
         table_sb = held.tile([P, V], BF16, name="table_sb")
         w_sb = held.tile([P, P], BF16, name="w_sb")
@@ -39,7 +39,7 @@ def tile_inductionheadattentionsmaller_kernel(tc, table, w, offs, out):
 
         h_bf = []
         for piece in range(PIECES):
-            h_ps = h_banks.tile([P, PIECE], F32, name=f"h_ps{piece}")
+            h_ps = banks.tile([P, PIECE], F32, name="h_ps", tag="bank")
             piece_offsets = offsets[:, piece * (PIECE // 16) : (piece + 1) * (PIECE // 16)]
             nc.tensor.matmul(h_ps[:], w_sb[:], table_sb[:].indirect(piece_offsets), start=True, stop=True)
             h_piece = held.tile([P, PIECE], BF16, name=f"h_bf{piece}")
@@ -52,7 +52,7 @@ def tile_inductionheadattentionsmaller_kernel(tc, table, w, offs, out):
         stored = 0
         for block in range(BLOCKS):
             for piece in range(PIECES):
-                scores = score_banks.tile([P, PIECE], F32, name=f"scores{piece}")
+                scores = banks.tile([P, PIECE], F32, name="scores", tag="bank")
                 nc.tensor.matmul(scores[:], table_blocks[:, block, :], h_bf[piece][:], start=True, stop=True)
                 leave_psum(piece, staged[:, block, piece * PIECE : (piece + 1) * PIECE], scores[:], SCALE)
             if block + 1 - stored == min(max(stored, 1), MAX_STORE):

@@ -13,6 +13,8 @@ PIECES = N // PIECE
 BLOCKS = V // P
 MAX_STORE = 4
 PSUM_BANKS = 8
+WARM_UP = 4
+WARM_UP_WIDTH = 512
 SCALE = math.sqrt(V) * ((V + 2) / V) ** 1.5 / 512
 
 FLOPS = 2 * P * P * N + 2 * P * V * N
@@ -30,6 +32,12 @@ def tile_inductionheadattentionsmaller_kernel(tc, table, w, offs, out):
         nc.sync.dma_start(table_sb[:], table)
         nc.sync.dma_start(w_sb[:], w)
         nc.sync.dma_start(offsets[:], offs)
+
+        zeros = held.tile([P, WARM_UP_WIDTH], BF16, name="zeros")
+        nc.vector.memset(zeros[:], 0.0)
+        warm = banks.tile([P, WARM_UP_WIDTH], F32, name="warm", tag="bank")
+        for repeat in range(WARM_UP):
+            nc.tensor.matmul(warm[:], zeros[:, :P], zeros[:], start=True, stop=True)
 
         def leave_psum(piece, dst, src, factor):
             if piece % 2 == 0:

@@ -13,8 +13,6 @@ PIECES = N // PIECE
 BLOCKS = V // P
 MAX_STORE = 4
 PSUM_BANKS = 8
-WARM_UP = 4
-WARM_UP_WIDTH = 512
 SCALE = math.sqrt(V) * ((V + 2) / V) ** 1.5 / 512
 
 FLOPS = 2 * P * P * N + 2 * P * V * N
@@ -32,12 +30,6 @@ def tile_inductionheadattentionsmaller_kernel(tc, table, w, offs, out):
         nc.sync.dma_start(table_sb[:], table)
         nc.sync.dma_start(w_sb[:], w)
         nc.sync.dma_start(offsets[:], offs)
-
-        zeros = held.tile([P, WARM_UP_WIDTH], BF16, name="zeros")
-        nc.vector.memset(zeros[:], 0.0)
-        warm = banks.tile([P, WARM_UP_WIDTH], F32, name="warm", tag="bank")
-        for repeat in range(WARM_UP):
-            nc.tensor.matmul(warm[:], zeros[:, :P], zeros[:], start=True, stop=True)
 
         def leave_psum(piece, dst, src, factor):
             if piece % 2 == 0:
@@ -63,6 +55,6 @@ def tile_inductionheadattentionsmaller_kernel(tc, table, w, offs, out):
                 scores = banks.tile([P, PIECE], F32, name="scores", tag="bank")
                 nc.tensor.matmul(scores[:], table_blocks[:, block, :], h_bf[piece][:], start=True, stop=True)
                 leave_psum(piece, staged[:, block, piece * PIECE : (piece + 1) * PIECE], scores[:], SCALE)
-            if block + 1 - stored == min(max(stored, 1), MAX_STORE):
+            if block + 1 - stored == min(max(stored, 1), max((BLOCKS - stored) // 2, 1), MAX_STORE):
                 nc.sync.dma_start(out_blocks[:, stored : block + 1, :], staged[:, stored : block + 1, :])
                 stored = block + 1

@@ -55,6 +55,12 @@ def tile_inductionheadattentionsmaller_kernel(tc, table, w, offs, out):
                 scores = banks.tile([P, PIECE], F32, name="scores", tag="bank")
                 nc.tensor.matmul(scores[:], table_blocks[:, block, :], h_bf[piece][:], start=True, stop=True)
                 leave_psum(piece, staged[:, block, piece * PIECE : (piece + 1) * PIECE], scores[:], SCALE)
+                if block == 0:
+                    tokens = slice(piece * PIECE, (piece + 1) * PIECE)
+                    nc.sync.dma_start(out_blocks[:, 0, tokens], staged[:, 0, tokens])
+            if block == 0:
+                stored = 1
+                continue
             if block + 1 - stored == min(max(stored, 1), max((BLOCKS - stored) // 2, 1), MAX_STORE):
                 nc.sync.dma_start(out_blocks[:, stored : block + 1, :], staged[:, stored : block + 1, :])
                 stored = block + 1

@@ -11,7 +11,6 @@ N = 1024
 PIECE = 256
 PIECES = N // PIECE
 BLOCKS = V // P
-MAX_STORE = 4
 PSUM_BANKS = 8
 SCALE = math.sqrt(V) * ((V + 2) / V) ** 1.5 / 512
 
@@ -61,6 +60,6 @@ def tile_inductionheadattentionsmaller_kernel(tc, table, w, offs, out):
             if block == 0:
                 stored = 1
                 continue
-            if block + 1 - stored == min(max(stored, 1), max((BLOCKS - stored) // 2, 1), MAX_STORE):
+            if block + 1 - stored == stored:
                 nc.sync.dma_start(out_blocks[:, stored : block + 1, :], staged[:, stored : block + 1, :])
                 stored = block + 1

@@ -8,8 +8,8 @@ COPY = mybir.ActivationFunctionType.Copy
 P = 128
 V = 2048
 N = 1024
-PIECE = 256
-PIECES = N // PIECE
+BANK = 512
+SHORT = 256
 BLOCKS = V // P
 PSUM_BANKS = 8
 SCALE = math.sqrt(V) * ((V + 2) / V) ** 1.5 / 512
@@ -36,26 +36,25 @@ def tile_inductionheadattentionsmaller_kernel(tc, table, w, offs, out):
             else:
                 nc.scalar.activation(dst, src, COPY, scale=factor)
 
-        h_bf = []
-        for piece in range(PIECES):
-            h_ps = banks.tile([P, PIECE], F32, name="h_ps", tag="bank")
-            piece_offsets = offsets[:, piece * (PIECE // 16) : (piece + 1) * (PIECE // 16)]
-            nc.tensor.matmul(h_ps[:], w_sb[:], table_sb[:].indirect(piece_offsets), start=True, stop=True)
-            h_piece = held.tile([P, PIECE], BF16, name=f"h_bf{piece}")
-            leave_psum(piece, h_piece[:], h_ps[:], 1.0)
-            h_bf.append(h_piece)
+        h_bf = held.tile([P, N], BF16, name="h_bf")
+        for piece in range(N // SHORT):
+            h_ps = banks.tile([P, BANK], F32, name="h_ps", tag="bank")
+            piece_offsets = offsets[:, piece * (SHORT // 16) : (piece + 1) * (SHORT // 16)]
+            nc.tensor.matmul(h_ps[:, :SHORT], w_sb[:], table_sb[:].indirect(piece_offsets), start=True, stop=True)
+            leave_psum(piece, h_bf[:, piece * SHORT : (piece + 1) * SHORT], h_ps[:, :SHORT], 1.0)
 
         table_blocks = table_sb[:].rearrange("k (p b) -> k b p", b=BLOCKS)
         out_blocks = out.rearrange("(p b) n -> p b n", b=BLOCKS)
         staged = held.tile([P, BLOCKS, N], F32, name="staged")
         stored = 0
         for block in range(BLOCKS):
-            for piece in range(PIECES):
-                scores = banks.tile([P, PIECE], F32, name="scores", tag="bank")
-                nc.tensor.matmul(scores[:], table_blocks[:, block, :], h_bf[piece][:], start=True, stop=True)
-                leave_psum(piece, staged[:, block, piece * PIECE : (piece + 1) * PIECE], scores[:], SCALE)
+            width = SHORT if block == 0 else BANK
+            for piece in range(N // width):
+                scores = banks.tile([P, BANK], F32, name="scores", tag="bank")
+                tokens = slice(piece * width, (piece + 1) * width)
+                nc.tensor.matmul(scores[:, :width], table_blocks[:, block, :], h_bf[:, tokens], start=True, stop=True)
+                leave_psum(piece, staged[:, block, tokens], scores[:, :width], SCALE)
                 if block == 0:
-                    tokens = slice(piece * PIECE, (piece + 1) * PIECE)
                     nc.sync.dma_start(out_blocks[:, 0, tokens], staged[:, 0, tokens])
             if block == 0:
                 stored = 1

@@ -47,6 +47,7 @@ def tile_inductionheadattentionsmaller_kernel(tc, table, w, offs, out):
         out_blocks = out.rearrange("(p b) n -> p b n", b=BLOCKS)
         staged = held.tile([P, BLOCKS, N], F32, name="staged")
         stored = 0
+        store_size = 1
         for block in range(BLOCKS):
             width = SHORT if block == 0 else BANK
             for piece in range(N // width):
@@ -59,6 +60,7 @@ def tile_inductionheadattentionsmaller_kernel(tc, table, w, offs, out):
             if block == 0:
                 stored = 1
                 continue
-            if block + 1 - stored == stored:
+            if block + 1 - stored == store_size:
                 nc.sync.dma_start(out_blocks[:, stored : block + 1, :], staged[:, stored : block + 1, :])
                 stored = block + 1
+                store_size += 1

@@ -47,7 +47,6 @@ def tile_inductionheadattentionsmaller_kernel(tc, table, w, offs, out):
         out_blocks = out.rearrange("(p b) n -> p b n", b=BLOCKS)
         staged = held.tile([P, BLOCKS, N], F32, name="staged")
         stored = 0
-        store_size = 1
         for block in range(BLOCKS):
             width = SHORT if block == 0 else BANK
             for piece in range(N // width):
@@ -60,7 +59,6 @@ def tile_inductionheadattentionsmaller_kernel(tc, table, w, offs, out):
             if block == 0:
                 stored = 1
                 continue
-            if block + 1 - stored == store_size:
+            if block + 1 - stored == max(stored // 2, 1) or block + 1 == BLOCKS:
                 nc.sync.dma_start(out_blocks[:, stored : block + 1, :], staged[:, stored : block + 1, :])
                 stored = block + 1
-                store_size += 1

@@ -11,6 +11,7 @@ N = 1024
 BANK = 512
 SHORT = 256
 BLOCKS = V // P
+EARLY = 3
 PSUM_BANKS = 8
 SCALE = math.sqrt(V) * ((V + 2) / V) ** 1.5 / 512
 
@@ -54,11 +55,11 @@ def tile_inductionheadattentionsmaller_kernel(tc, table, w, offs, out):
                 tokens = slice(piece * width, (piece + 1) * width)
                 nc.tensor.matmul(scores[:, :width], table_blocks[:, block, :], h_bf[:, tokens], start=True, stop=True)
                 leave_psum(piece, staged[:, block, tokens], scores[:, :width], SCALE)
-                if block == 0:
-                    nc.sync.dma_start(out_blocks[:, 0, tokens], staged[:, 0, tokens])
-            if block == 0:
-                stored = 1
+                if block < EARLY:
+                    nc.sync.dma_start(out_blocks[:, block, tokens], staged[:, block, tokens])
+            if block < EARLY:
+                stored = block + 1
                 continue
-            if block + 1 - stored == max(stored // 2, 1) or block + 1 == BLOCKS:
+            if block + 1 - stored == stored // 2 or block + 1 == BLOCKS:
                 nc.sync.dma_start(out_blocks[:, stored : block + 1, :], staged[:, stored : block + 1, :])
                 stored = block + 1

import math

import concourse.mybir as mybir

BF16, F32, U16 = mybir.dt.bfloat16, mybir.dt.float32, mybir.dt.uint16
COPY = mybir.ActivationFunctionType.Copy

P = 128
V = 2048
N = 1024
BANK = 512
SHORT = 256
BLOCKS = V // P
EARLY = 3
PSUM_BANKS = 8
SCALE = math.sqrt(V) * ((V + 2) / V) ** 1.5 / 512

FLOPS = 2 * P * P * N + 2 * P * V * N


def tile_inductionheadattentionsmaller_kernel(tc, table, w, offs, out):
    nc = tc.nc
    with (
        tc.tile_pool(name="held", bufs=1) as held,
        tc.psum_pool(name="banks", bufs=PSUM_BANKS) as banks,
    ):
        table_sb = held.tile([P, V], BF16, name="table_sb")
        w_sb = held.tile([P, P], BF16, name="w_sb")
        offsets = held.tile([P, N // 16], U16, name="offsets")
        nc.sync.dma_start(table_sb[:], table)
        nc.sync.dma_start(w_sb[:], w)
        nc.sync.dma_start(offsets[:], offs)

        def leave_psum(piece, dst, src, factor):
            if piece % 2 == 0:
                nc.vector.tensor_scalar_mul(dst, src, factor)
            else:
                nc.scalar.activation(dst, src, COPY, scale=factor)

        h_bf = held.tile([P, N], BF16, name="h_bf")
        for piece in range(N // SHORT):
            h_ps = banks.tile([P, BANK], F32, name="h_ps", tag="bank")
            piece_offsets = offsets[:, piece * (SHORT // 16) : (piece + 1) * (SHORT // 16)]
            nc.tensor.matmul(h_ps[:, :SHORT], w_sb[:], table_sb[:].indirect(piece_offsets), start=True, stop=True)
            leave_psum(piece, h_bf[:, piece * SHORT : (piece + 1) * SHORT], h_ps[:, :SHORT], 1.0)

        table_blocks = table_sb[:].rearrange("k (p b) -> k b p", b=BLOCKS)
        out_blocks = out.rearrange("(p b) n -> p b n", b=BLOCKS)
        staged = held.tile([P, BLOCKS, N], F32, name="staged")
        stored = 0
        for block in range(BLOCKS):
            width = SHORT if block == 0 else BANK
            for piece in range(N // width):
                scores = banks.tile([P, BANK], F32, name="scores", tag="bank")
                tokens = slice(piece * width, (piece + 1) * width)
                nc.tensor.matmul(scores[:, :width], table_blocks[:, block, :], h_bf[:, tokens], start=True, stop=True)
                leave_psum(piece, staged[:, block, tokens], scores[:, :width], SCALE)
                if block < EARLY:
                    nc.sync.dma_start(out_blocks[:, block, tokens], staged[:, block, tokens])
            if block < EARLY:
                stored = block + 1
                continue
            if block + 1 - stored == stored // 2 or block + 1 == BLOCKS:
                nc.sync.dma_start(out_blocks[:, stored : block + 1, :], staged[:, stored : block + 1, :])
                stored = block + 1
